import numpy as np
import ml_dtypes


def mxq(x, axis, fmt="e4m3"):
    dtype, down = {"e4m3": (ml_dtypes.float8_e4m3fn, 7), "e5m2": (ml_dtypes.float8_e5m2, 14)}[fmt]
    v = np.moveaxis(np.asarray(x, np.float32).astype(ml_dtypes.bfloat16).astype(np.float64), axis, -1)
    blocks = v.reshape(v.shape[:-1] + (-1, 32))
    amax = np.abs(blocks).max(-1, keepdims=True)
    byte = np.maximum(np.where(amax > 0, np.frexp(amax)[1] - 1 + 127, 0) - down, 1)
    scale = np.exp2(byte - 127.0)
    codes = (blocks / scale).astype(np.float32).astype(dtype).astype(np.float64)
    return np.moveaxis((codes * scale).reshape(v.shape), -1, axis)


WIDE = False


def mx_kscale(k):
    if not WIDE:
        return np.ones(k)
    levels = np.array([10, -10, 5, -5, 0])
    if k % 512:
        return np.exp2(np.random.permutation(np.resize(levels, k // 32))).repeat(32)
    a = np.empty((k // 512, 16))
    for p in range(k // 512):
        a[p, :8] = np.random.permutation(np.resize(levels, 8))
        for g in range(8):
            far = levels[np.abs(levels - a[p, g]) >= 10]
            a[p, g + 8] = far[np.random.randint(len(far))]
    return np.exp2(a.ravel()).repeat(32)


BF16 = ml_dtypes.bfloat16


def bf(x):
    return np.asarray(x, np.float32).astype(BF16)


def f64(x):
    return np.asarray(x).astype(np.float64)


B, D, K = 5120, 512, 2


def setup_inputs():
    s = mx_kscale(D)
    x = np.random.standard_normal((B, D, K)) * s[None, :, None]
    mu = np.random.standard_normal((D, K)) * 0.3 * s[:, None]
    w = (np.eye(D)[None] + np.random.standard_normal((K, D, D)) * 0.7 / np.sqrt(D)) / s[None, None, :]
    return {"x": bf(x), "mu_track": bf(mu), "Std_inv_track": bf(w)}


def reference(x, mu_track, Std_inv_track):
    x_cnt = f64(x) - f64(mu_track)[None]
    xq = mxq(x_cnt, 1, "e4m3")
    wq = mxq(f64(Std_inv_track), 2, "e4m3")
    z = wq @ xq.transpose(2, 1, 0)
    return z.transpose(2, 1, 0)

@@ -1,0 +1,235 @@
+from contextlib import ExitStack
+
+import concourse.mybir as mybir
+from concourse.masks import make_identity
+
+F32 = mybir.dt.float32
+BF16 = mybir.dt.bfloat16
+U32 = mybir.dt.uint32
+U8 = mybir.dt.uint8
+FP8X4 = mybir.dt.float8_e4m3fn_x4
+ALU = mybir.AluOpType
+
+P = 128
+B, D, K = 5120, 512, 2
+T = D // P
+H = D // 2
+NT = B // P
+NP = NT // 2
+FLOPS = 2 * B * D * D * K
+
+X_CHUNKS = [1, 1, 2, 4, 8, 8, 16]
+O_CHUNKS = [4, 4, 4, 4, 4, 4, 4, 4, 4, 2, 2]
+O_MAX = 4
+O_BUFS = 6
+
+
+def tile_clusternorm1dv3_t_kernel(tc, x, mu_track, Std_inv_track, out):
+    nc = tc.nc
+    assert sum(X_CHUNKS) == NT and sum(O_CHUNKS) == NT
+
+    xv = x.rearrange("(p j) e k -> p j (e k)", j=NT)
+    ov = out.rearrange("(p j) d k -> p j (d k)", j=NT)
+    wv = Std_inv_track.rearrange("k (p c) e -> k p c e", c=T)
+    muv = mu_track.rearrange("(p t) k -> p (t k)", t=T)
+
+    with ExitStack() as ctx:
+        keep = ctx.enter_context(tc.tile_pool(name="keep", bufs=1))
+        rpool = ctx.enter_context(tc.tile_pool(name="rpool", bufs=2))
+        gpool = ctx.enter_context(tc.tile_pool(name="gpool", bufs=3))
+        cpool = ctx.enter_context(tc.tile_pool(name="cpool", bufs=3))
+        opool = ctx.enter_context(tc.tile_pool(name="opool", bufs=O_BUFS))
+        psum_t = ctx.enter_context(tc.psum_pool(name="psum_t", bufs=4))
+        psum_o = ctx.enter_context(tc.psum_pool(name="psum_o", bufs=4))
+
+        mu_w = keep.tile([P, T * K], BF16, name="mu_w")
+
+        x_tiles = []
+        x_loads = []
+        j0 = 0
+        for ci, n in enumerate(X_CHUNKS):
+            x_sb = keep.tile([P, n, D * K], BF16, name="x_sb%d" % ci)
+            x_loads.append((x_sb, j0, n))
+            for jj in range(n):
+                x_tiles.append((x_sb, jj))
+            j0 += n
+        w_sb = [keep.tile([P, T, D], BF16, name="w_sb%d" % k) for k in range(K)]
+
+        def load_x(ci):
+            x_sb, a, n = x_loads[ci]
+            nc.sync.dma_start(out=x_sb[:], in_=xv[:, a : a + n, :])
+
+        load_x(0)
+        nc.sync.dma_start(out=mu_w[:], in_=muv)
+        load_x(1)
+        nc.sync.dma_start(out=w_sb[0][:], in_=wv[0])
+        nc.sync.dma_start(out=w_sb[1][:], in_=wv[1])
+        for ci in range(2, len(X_CHUNKS)):
+            load_x(ci)
+
+        ident_f = keep.tile([P, P], F32, name="ident_f")
+        make_identity(nc, ident_f[:])
+        ident_b = keep.tile([P, P], BF16, name="ident_b")
+        make_identity(nc, ident_b[:])
+
+        w_grp = [keep.tile([P, D, T], BF16, name="w_grp%d" % k, align_bytes=64) for k in range(K)]
+        w_codes = keep.tile([P, K, D], U32, name="w_codes", align_bytes=64)
+        w_scales = keep.tile([P, K, D], U8, name="w_scales", align_bytes=64)
+
+        mu_sb = mu_w[:].rearrange("p (t k) -> p t k", k=K)
+        mu_kbt = mu_sb.rearrange("p t k -> p k t").unsqueeze(2).to_broadcast([P, K, P, T])
+        mu_tbk = mu_sb.unsqueeze(2).to_broadcast([P, T, P, K])
+
+        xt_of = {}
+        xr_of = {}
+        xg_of = {}
+        xq_of = {}
+
+        def transposes(j):
+            x_sb, jj = x_tiles[j]
+            words = x_sb[:].bitcast(F32)
+            xt = psum_t.tile([P, T, P], F32, name="xt", tag="xt")
+            for t in range(T):
+                nc.tensor.transpose(xt[:, t, :], words[:, jj, t:D:T], ident_f[:])
+            xt_of[j] = xt
+
+        def pair_tile(n):
+            if n not in xg_of:
+                xg_of[n] = gpool.tile([P, 2, K, P, T], BF16, name="xg", tag="xg", align_bytes=64)
+            return xg_of[n]
+
+        def centre_and_regroup(j):
+            nc.vector.tensor_tensor(
+                out=pair_tile(j // 2)[:, 1],
+                in0=xt_of[j][:].bitcast(BF16).rearrange("p t (b k) -> p k b t", k=K),
+                in1=mu_kbt,
+                op=ALU.subtract,
+            )
+
+        def centre_only(j):
+            xr = rpool.tile([P, T, P, K], BF16, name="xr", tag="xr")
+            nc.vector.tensor_tensor(
+                out=xr[:],
+                in0=xt_of[j][:].bitcast(BF16).rearrange("p t (b k) -> p t b k", k=K),
+                in1=mu_tbk,
+                op=ALU.subtract,
+            )
+            xr_of[j] = xr
+
+        def regroup(j):
+            dst = pair_tile(j // 2)[:, 0]
+            src = xr_of[j][:].rearrange("p t b k -> p k b t")
+            nc.gpsimd.tensor_scalar(out=dst, in0=src, scalar1=1.0, scalar2=0.0, op0=ALU.mult, op1=ALU.add)
+
+        def quantise(n):
+            xc = cpool.tile([P, 2 * K * P], U32, name="xc", tag="xc", align_bytes=64)
+            xs = cpool.tile([P, 2 * K * P], U8, name="xs", tag="xs", align_bytes=64)
+            nc.vector.quantize_mx(
+                out=xc[:].bitcast(FP8X4),
+                scales=xs[:],
+                in_=xg_of[n][:].rearrange("p s k b t -> p (s k b t)"),
+            )
+            xq_of[n] = (xc, xs)
+
+        o_state = {"chunk": 0, "fill": 0, "start": 0, "tile": None}
+
+        def multiply(n):
+            xc, xs = xq_of[n]
+            banks = []
+            for s in range(2):
+                po = [psum_o.tile([P, K, H], F32, name="po", tag="po") for h in range(2)]
+                for k in range(K):
+                    c0 = (s * K + k) * P
+                    for h in range(2):
+                        nc.tensor.matmul_mx(
+                            out=po[h][:, k, :],
+                            lhsT=xc[:, c0 : c0 + P].bitcast(FP8X4),
+                            lhsT_scale=xs[:, c0 : c0 + P],
+                            rhs=w_codes[:, k, h * H : (h + 1) * H].bitcast(FP8X4),
+                            rhs_scale=w_scales[:, k, h * H : (h + 1) * H],
+                            start=True,
+                            stop=True,
+                        )
+                banks.append(po)
+            return banks
+
+        def drain(banks, engines):
+            for s in range(2):
+                if o_state["fill"] == 0:
+                    o_state["tile"] = opool.tile([P, O_MAX, D * K], F32, name="o_sb", tag="o_sb")
+                o_sb = o_state["tile"]
+                jj = o_state["fill"]
+                for h in range(2):
+                    dst = o_sb[:, jj, h * H * K : (h + 1) * H * K].rearrange("p (d k) -> p d k", k=K)
+                    src = banks[s][h][:].rearrange("p k d -> p d k")
+                    if engines[s] == "v":
+                        nc.vector.tensor_copy(out=dst, in_=src)
+                    else:
+                        nc.scalar.copy(out=dst, in_=src)
+                o_state["fill"] += 1
+                n = O_CHUNKS[o_state["chunk"]]
+                if o_state["fill"] == n:
+                    a = o_state["start"]
+                    nc.sync.dma_start(out=ov[:, a : a + n, :], in_=o_sb[:, 0:n, :])
+                    o_state["start"] = a + n
+                    o_state["chunk"] += 1
+                    o_state["fill"] = 0
+
+        def w_transposes(k):
+            banks = []
+            for cp in range(2):
+                wt = psum_o.tile([P, 2, T, P], BF16, name="wt", tag="po")
+                for c2 in range(2):
+                    for t in range(T):
+                        nc.tensor.transpose(
+                            wt[:, c2, t, :], w_sb[k][:, 2 * cp + c2, t:D:T], ident_b[:]
+                        )
+                banks.append(wt)
+            return banks
+
+        def w_copy(k, cp, wt, engine):
+            dst = w_grp[k][:].rearrange("p (q a c) t -> p q a (c t)", a=2, c=2)[:, :, cp, :]
+            src = wt[:].rearrange("p c t q -> p q (c t)")
+            if engine == "v":
+                nc.vector.tensor_copy(out=dst, in_=src)
+            else:
+                nc.scalar.copy(out=dst, in_=src)
+
+        def w_quant(k):
+            nc.vector.quantize_mx(
+                out=w_codes[:, k, :].bitcast(FP8X4),
+                scales=w_scales[:, k, :],
+                in_=w_grp[k][:].rearrange("p d t -> p (d t)"),
+            )
+
+        transposes(0)
+        transposes(1)
+        centre_only(0)
+        regroup(0)
+        wt0 = w_transposes(0)
+        centre_and_regroup(1)
+        w_copy(0, 0, wt0[0], "v")
+        w_copy(0, 1, wt0[1], "v")
+        wt1 = w_transposes(1)
+        w_copy(1, 0, wt1[0], "s")
+        w_copy(1, 1, wt1[1], "s")
+        transposes(2)
+        transposes(3)
+        w_quant(0)
+        centre_only(2)
+        regroup(2)
+        w_quant(1)
+        transposes(4)
+        transposes(5)
+        quantise(0)
+        drain(multiply(0), "ss")
+        for n in range(1, NP):
+            centre_and_regroup(2 * n + 1)
+            if n + 1 < NP:
+                centre_only(2 * n + 2)
+                regroup(2 * n + 2)
+            if n + 2 < NP:
+                transposes(2 * n + 4)
+                transposes(2 * n + 5)
+            quantise(n)
+            drain(multiply(n), "sv" if n == NP - 1 else "ss")

@@ -19,9 +19,8 @@ NP = NT // 2
 FLOPS = 2 * B * D * D * K
 
 X_CHUNKS = [1, 1, 2, 4, 8, 8, 16]
-O_CHUNKS = [4, 4, 4, 4, 4, 4, 4, 4, 4, 2, 2]
-O_MAX = 4
-O_BUFS = 6
+O_CHUNKS = [8, 8, 8, 4, 4, 4, 2, 2]
+RING = 28
 
 
 def tile_clusternorm1dv3_t_kernel(tc, x, mu_track, Std_inv_track, out):
@@ -38,7 +37,6 @@ def tile_clusternorm1dv3_t_kernel(tc, x, mu_track, Std_inv_track, out):
         rpool = ctx.enter_context(tc.tile_pool(name="rpool", bufs=2))
         gpool = ctx.enter_context(tc.tile_pool(name="gpool", bufs=3))
         cpool = ctx.enter_context(tc.tile_pool(name="cpool", bufs=3))
-        opool = ctx.enter_context(tc.tile_pool(name="opool", bufs=O_BUFS))
         psum_t = ctx.enter_context(tc.psum_pool(name="psum_t", bufs=4))
         psum_o = ctx.enter_context(tc.psum_pool(name="psum_o", bufs=4))
 
@@ -69,8 +67,6 @@ def tile_clusternorm1dv3_t_kernel(tc, x, mu_track, Std_inv_track, out):
 
         ident_f = keep.tile([P, P], F32, name="ident_f")
         make_identity(nc, ident_f[:])
-        ident_b = keep.tile([P, P], BF16, name="ident_b")
-        make_identity(nc, ident_b[:])
 
         w_grp = [keep.tile([P, D, T], BF16, name="w_grp%d" % k, align_bytes=64) for k in range(K)]
         w_codes = keep.tile([P, K, D], U32, name="w_codes", align_bytes=64)
@@ -131,7 +127,8 @@ def tile_clusternorm1dv3_t_kernel(tc, x, mu_track, Std_inv_track, out):
             )
             xq_of[n] = (xc, xs)
 
-        o_state = {"chunk": 0, "fill": 0, "start": 0, "tile": None}
+        ring = keep.tile([P, RING, D * K], F32, name="ring")
+        o_state = {"chunk": 0, "fill": 0, "start": 0}
 
         def multiply(n):
             xc, xs = xq_of[n]
@@ -155,14 +152,11 @@ def tile_clusternorm1dv3_t_kernel(tc, x, mu_track, Std_inv_track, out):
 
         def drain(banks, engines):
             for s in range(2):
-                if o_state["fill"] == 0:
-                    o_state["tile"] = opool.tile([P, O_MAX, D * K], F32, name="o_sb", tag="o_sb")
-                o_sb = o_state["tile"]
-                jj = o_state["fill"]
+                jj = (o_state["start"] + o_state["fill"]) % RING
                 for h in range(2):
-                    dst = o_sb[:, jj, h * H * K : (h + 1) * H * K].rearrange("p (d k) -> p d k", k=K)
+                    dst = ring[:, jj, h * H * K : (h + 1) * H * K].rearrange("p (d k) -> p d k", k=K)
                     src = banks[s][h][:].rearrange("p k d -> p d k")
-                    if engines[s] == "v":
+                    if engines[2 * s + h] == "v":
                         nc.vector.tensor_copy(out=dst, in_=src)
                     else:
                         nc.scalar.copy(out=dst, in_=src)
@@ -170,26 +164,27 @@ def tile_clusternorm1dv3_t_kernel(tc, x, mu_track, Std_inv_track, out):
                 n = O_CHUNKS[o_state["chunk"]]
                 if o_state["fill"] == n:
                     a = o_state["start"]
-                    nc.sync.dma_start(out=ov[:, a : a + n, :], in_=o_sb[:, 0:n, :])
+                    r0 = a % RING
+                    nc.sync.dma_start(out=ov[:, a : a + n, :], in_=ring[:, r0 : r0 + n, :])
                     o_state["start"] = a + n
                     o_state["chunk"] += 1
                     o_state["fill"] = 0
 
         def w_transposes(k):
+            words = w_sb[k][:].bitcast(F32)
             banks = []
             for cp in range(2):
-                wt = psum_o.tile([P, 2, T, P], BF16, name="wt", tag="po")
+                wt = psum_o.tile([P, 2, 2, P], F32, name="wt", tag="po")
                 for c2 in range(2):
-                    for t in range(T):
-                        nc.tensor.transpose(
-                            wt[:, c2, t, :], w_sb[k][:, 2 * cp + c2, t:D:T], ident_b[:]
-                        )
+                    for u in range(2):
+                        nc.tensor.transpose(wt[:, c2, u, :], words[:, 2 * cp + c2, u : D // 2 : 2], ident_f[:])
                 banks.append(wt)
             return banks
 
         def w_copy(k, cp, wt, engine):
-            dst = w_grp[k][:].rearrange("p (q a c) t -> p q a (c t)", a=2, c=2)[:, :, cp, :]
-            src = wt[:].rearrange("p c t q -> p q (c t)")
+            dst = w_grp[k][:].rearrange("p d t -> p (d t)").bitcast(F32)
+            dst = dst.rearrange("p (q a w) -> p q a w", a=2, w=4)[:, :, cp, :]
+            src = wt[:].rearrange("p c u q -> p q (c u)")
             if engine == "v":
                 nc.vector.tensor_copy(out=dst, in_=src)
             else:
@@ -202,34 +197,36 @@ def tile_clusternorm1dv3_t_kernel(tc, x, mu_track, Std_inv_track, out):
                 in_=w_grp[k][:].rearrange("p d t -> p (d t)"),
             )
 
+        ctx.enter_context(tc.manual_schedule())
         transposes(0)
         transposes(1)
         centre_only(0)
         regroup(0)
-        wt0 = w_transposes(0)
         centre_and_regroup(1)
+        wt0 = w_transposes(0)
         w_copy(0, 0, wt0[0], "v")
-        w_copy(0, 1, wt0[1], "v")
+        w_copy(0, 1, wt0[1], "s")
         wt1 = w_transposes(1)
         w_copy(1, 0, wt1[0], "s")
         w_copy(1, 1, wt1[1], "s")
         transposes(2)
         transposes(3)
         w_quant(0)
-        centre_only(2)
-        regroup(2)
-        w_quant(1)
-        transposes(4)
-        transposes(5)
         quantise(0)
-        drain(multiply(0), "ss")
-        for n in range(1, NP):
-            centre_and_regroup(2 * n + 1)
+        w_quant(1)
+        for n in range(NP):
             if n + 1 < NP:
                 centre_only(2 * n + 2)
                 regroup(2 * n + 2)
-            if n + 2 < NP:
-                transposes(2 * n + 4)
-                transposes(2 * n + 5)
-            quantise(n)
-            drain(multiply(n), "sv" if n == NP - 1 else "ss")
+            if n > 0:
+                quantise(n)
+            if n + 1 < NP:
+                centre_and_regroup(2 * n + 3)
+            banks = multiply(n)
+            if n == 0:
+                transposes(4)
+                transposes(5)
+            if n + 3 < NP:
+                transposes(2 * n + 6)
+                transposes(2 * n + 7)
+            drain(banks, "svsv" if n == NP - 1 else "ssss")

@@ -19,7 +19,7 @@ NP = NT // 2
 FLOPS = 2 * B * D * D * K
 
 X_CHUNKS = [1, 1, 2, 4, 8, 8, 16]
-O_CHUNKS = [8, 8, 8, 4, 4, 4, 2, 2]
+O_CHUNKS = [4, 4, 4, 4, 4, 4, 4, 4, 4, 2, 2]
 RING = 28
 
 

@@ -18,7 +18,7 @@ NT = B // P
 NP = NT // 2
 FLOPS = 2 * B * D * D * K
 
-X_CHUNKS = [1, 1, 2, 4, 8, 8, 16]
+X_CHUNKS = [2, 2, 4, 8, 24]
 O_CHUNKS = [4, 4, 4, 4, 4, 4, 4, 4, 4, 2, 2]
 RING = 28
 
@@ -30,7 +30,7 @@ def tile_clusternorm1dv3_t_kernel(tc, x, mu_track, Std_inv_track, out):
     xv = x.rearrange("(p j) e k -> p j (e k)", j=NT)
     ov = out.rearrange("(p j) d k -> p j (d k)", j=NT)
     wv = Std_inv_track.rearrange("k (p c) e -> k p c e", c=T)
-    muv = mu_track.rearrange("(p t) k -> p (t k)", t=T)
+    muv = mu_track.rearrange("(o e) k -> o (e k)", o=1)
 
     with ExitStack() as ctx:
         keep = ctx.enter_context(tc.tile_pool(name="keep", bufs=1))
@@ -40,7 +40,8 @@ def tile_clusternorm1dv3_t_kernel(tc, x, mu_track, Std_inv_track, out):
         psum_t = ctx.enter_context(tc.psum_pool(name="psum_t", bufs=4))
         psum_o = ctx.enter_context(tc.psum_pool(name="psum_o", bufs=4))
 
-        mu_w = keep.tile([P, T * K], BF16, name="mu_w")
+        mu_row = keep.tile([P, D], F32, name="mu_row")
+        nc.vector.memset(mu_row[:], 0.0)
 
         x_tiles = []
         x_loads = []
@@ -58,11 +59,10 @@ def tile_clusternorm1dv3_t_kernel(tc, x, mu_track, Std_inv_track, out):
             nc.sync.dma_start(out=x_sb[:], in_=xv[:, a : a + n, :])
 
         load_x(0)
-        nc.sync.dma_start(out=mu_w[:], in_=muv)
-        load_x(1)
+        nc.sync.dma_start(out=mu_row[0:1, :].bitcast(BF16), in_=muv)
         nc.sync.dma_start(out=w_sb[0][:], in_=wv[0])
         nc.sync.dma_start(out=w_sb[1][:], in_=wv[1])
-        for ci in range(2, len(X_CHUNKS)):
+        for ci in range(1, len(X_CHUNKS)):
             load_x(ci)
 
         ident_f = keep.tile([P, P], F32, name="ident_f")
@@ -72,7 +72,8 @@ def tile_clusternorm1dv3_t_kernel(tc, x, mu_track, Std_inv_track, out):
         w_codes = keep.tile([P, K, D], U32, name="w_codes", align_bytes=64)
         w_scales = keep.tile([P, K, D], U8, name="w_scales", align_bytes=64)
 
-        mu_sb = mu_w[:].rearrange("p (t k) -> p t k", k=K)
+        mu_w = keep.tile([P, T], F32, name="mu_w")
+        mu_sb = mu_w[:].bitcast(BF16).rearrange("p (t k) -> p t k", k=K)
         mu_kbt = mu_sb.rearrange("p t k -> p k t").unsqueeze(2).to_broadcast([P, K, P, T])
         mu_tbk = mu_sb.unsqueeze(2).to_broadcast([P, T, P, K])
 
@@ -88,6 +89,12 @@ def tile_clusternorm1dv3_t_kernel(tc, x, mu_track, Std_inv_track, out):
             for t in range(T):
                 nc.tensor.transpose(xt[:, t, :], words[:, jj, t:D:T], ident_f[:])
             xt_of[j] = xt
+
+        def spread_mu():
+            mt = psum_t.tile([P, T, P], F32, name="mt", tag="xt")
+            for t in range(T):
+                nc.tensor.transpose(mt[:, t, :], mu_row[:, t:D:T], ident_f[:])
+            nc.vector.tensor_copy(out=mu_w[:], in_=mt[:, :, 0])
 
         def pair_tile(n):
             if n not in xg_of:
@@ -199,6 +206,7 @@ def tile_clusternorm1dv3_t_kernel(tc, x, mu_track, Std_inv_track, out):
 
         ctx.enter_context(tc.manual_schedule())
         transposes(0)
+        spread_mu()
         transposes(1)
         centre_only(0)
         regroup(0)

from contextlib import ExitStack

import concourse.mybir as mybir
from concourse.masks import make_identity

F32 = mybir.dt.float32
BF16 = mybir.dt.bfloat16
U32 = mybir.dt.uint32
U8 = mybir.dt.uint8
FP8X4 = mybir.dt.float8_e4m3fn_x4
ALU = mybir.AluOpType

P = 128
B, D, K = 5120, 512, 2
T = D // P
H = D // 2
NT = B // P
NP = NT // 2
FLOPS = 2 * B * D * D * K

X_CHUNKS = [2, 2, 4, 8, 24]
O_CHUNKS = [4, 4, 4, 4, 4, 4, 4, 4, 4, 2, 2]
RING = 28


def tile_clusternorm1dv3_t_kernel(tc, x, mu_track, Std_inv_track, out):
    nc = tc.nc
    assert sum(X_CHUNKS) == NT and sum(O_CHUNKS) == NT

    xv = x.rearrange("(p j) e k -> p j (e k)", j=NT)
    ov = out.rearrange("(p j) d k -> p j (d k)", j=NT)
    wv = Std_inv_track.rearrange("k (p c) e -> k p c e", c=T)
    muv = mu_track.rearrange("(o e) k -> o (e k)", o=1)

    with ExitStack() as ctx:
        keep = ctx.enter_context(tc.tile_pool(name="keep", bufs=1))
        rpool = ctx.enter_context(tc.tile_pool(name="rpool", bufs=2))
        gpool = ctx.enter_context(tc.tile_pool(name="gpool", bufs=3))
        cpool = ctx.enter_context(tc.tile_pool(name="cpool", bufs=3))
        psum_t = ctx.enter_context(tc.psum_pool(name="psum_t", bufs=4))
        psum_o = ctx.enter_context(tc.psum_pool(name="psum_o", bufs=4))

        mu_row = keep.tile([P, D], F32, name="mu_row")
        nc.vector.memset(mu_row[:], 0.0)

        x_tiles = []
        x_loads = []
        j0 = 0
        for ci, n in enumerate(X_CHUNKS):
            x_sb = keep.tile([P, n, D * K], BF16, name="x_sb%d" % ci)
            x_loads.append((x_sb, j0, n))
            for jj in range(n):
                x_tiles.append((x_sb, jj))
            j0 += n
        w_sb = [keep.tile([P, T, D], BF16, name="w_sb%d" % k) for k in range(K)]

        def load_x(ci):
            x_sb, a, n = x_loads[ci]
            nc.sync.dma_start(out=x_sb[:], in_=xv[:, a : a + n, :])

        load_x(0)
        nc.sync.dma_start(out=mu_row[0:1, :].bitcast(BF16), in_=muv)
        nc.sync.dma_start(out=w_sb[0][:], in_=wv[0])
        nc.sync.dma_start(out=w_sb[1][:], in_=wv[1])
        for ci in range(1, len(X_CHUNKS)):
            load_x(ci)

        ident_f = keep.tile([P, P], F32, name="ident_f")
        make_identity(nc, ident_f[:])

        w_grp = [keep.tile([P, D, T], BF16, name="w_grp%d" % k, align_bytes=64) for k in range(K)]
        w_codes = keep.tile([P, K, D], U32, name="w_codes", align_bytes=64)
        w_scales = keep.tile([P, K, D], U8, name="w_scales", align_bytes=64)

        mu_w = keep.tile([P, T], F32, name="mu_w")
        mu_sb = mu_w[:].bitcast(BF16).rearrange("p (t k) -> p t k", k=K)
        mu_kbt = mu_sb.rearrange("p t k -> p k t").unsqueeze(2).to_broadcast([P, K, P, T])
        mu_tbk = mu_sb.unsqueeze(2).to_broadcast([P, T, P, K])

        xt_of = {}
        xr_of = {}
        xg_of = {}
        xq_of = {}

        def transposes(j):
            x_sb, jj = x_tiles[j]
            words = x_sb[:].bitcast(F32)
            xt = psum_t.tile([P, T, P], F32, name="xt", tag="xt")
            for t in range(T):
                nc.tensor.transpose(xt[:, t, :], words[:, jj, t:D:T], ident_f[:])
            xt_of[j] = xt

        def spread_mu():
            mt = psum_t.tile([P, T, P], F32, name="mt", tag="xt")
            for t in range(T):
                nc.tensor.transpose(mt[:, t, :], mu_row[:, t:D:T], ident_f[:])
            nc.vector.tensor_copy(out=mu_w[:], in_=mt[:, :, 0])

        def pair_tile(n):
            if n not in xg_of:
                xg_of[n] = gpool.tile([P, 2, K, P, T], BF16, name="xg", tag="xg", align_bytes=64)
            return xg_of[n]

        def centre_and_regroup(j):
            nc.vector.tensor_tensor(
                out=pair_tile(j // 2)[:, 1],
                in0=xt_of[j][:].bitcast(BF16).rearrange("p t (b k) -> p k b t", k=K),
                in1=mu_kbt,
                op=ALU.subtract,
            )

        def centre_only(j):
            xr = rpool.tile([P, T, P, K], BF16, name="xr", tag="xr")
            nc.vector.tensor_tensor(
                out=xr[:],
                in0=xt_of[j][:].bitcast(BF16).rearrange("p t (b k) -> p t b k", k=K),
                in1=mu_tbk,
                op=ALU.subtract,
            )
            xr_of[j] = xr

        def regroup(j):
            dst = pair_tile(j // 2)[:, 0]
            src = xr_of[j][:].rearrange("p t b k -> p k b t")
            nc.gpsimd.tensor_scalar(out=dst, in0=src, scalar1=1.0, scalar2=0.0, op0=ALU.mult, op1=ALU.add)

        def quantise(n):
            xc = cpool.tile([P, 2 * K * P], U32, name="xc", tag="xc", align_bytes=64)
            xs = cpool.tile([P, 2 * K * P], U8, name="xs", tag="xs", align_bytes=64)
            nc.vector.quantize_mx(
                out=xc[:].bitcast(FP8X4),
                scales=xs[:],
                in_=xg_of[n][:].rearrange("p s k b t -> p (s k b t)"),
            )
            xq_of[n] = (xc, xs)

        ring = keep.tile([P, RING, D * K], F32, name="ring")
        o_state = {"chunk": 0, "fill": 0, "start": 0}

        def multiply(n):
            xc, xs = xq_of[n]
            banks = []
            for s in range(2):
                po = [psum_o.tile([P, K, H], F32, name="po", tag="po") for h in range(2)]
                for k in range(K):
                    c0 = (s * K + k) * P
                    for h in range(2):
                        nc.tensor.matmul_mx(
                            out=po[h][:, k, :],
                            lhsT=xc[:, c0 : c0 + P].bitcast(FP8X4),
                            lhsT_scale=xs[:, c0 : c0 + P],
                            rhs=w_codes[:, k, h * H : (h + 1) * H].bitcast(FP8X4),
                            rhs_scale=w_scales[:, k, h * H : (h + 1) * H],
                            start=True,
                            stop=True,
                        )
                banks.append(po)
            return banks

        def drain(banks, engines):
            for s in range(2):
                jj = (o_state["start"] + o_state["fill"]) % RING
                for h in range(2):
                    dst = ring[:, jj, h * H * K : (h + 1) * H * K].rearrange("p (d k) -> p d k", k=K)
                    src = banks[s][h][:].rearrange("p k d -> p d k")
                    if engines[2 * s + h] == "v":
                        nc.vector.tensor_copy(out=dst, in_=src)
                    else:
                        nc.scalar.copy(out=dst, in_=src)
                o_state["fill"] += 1
                n = O_CHUNKS[o_state["chunk"]]
                if o_state["fill"] == n:
                    a = o_state["start"]
                    r0 = a % RING
                    nc.sync.dma_start(out=ov[:, a : a + n, :], in_=ring[:, r0 : r0 + n, :])
                    o_state["start"] = a + n
                    o_state["chunk"] += 1
                    o_state["fill"] = 0

        def w_transposes(k):
            words = w_sb[k][:].bitcast(F32)
            banks = []
            for cp in range(2):
                wt = psum_o.tile([P, 2, 2, P], F32, name="wt", tag="po")
                for c2 in range(2):
                    for u in range(2):
                        nc.tensor.transpose(wt[:, c2, u, :], words[:, 2 * cp + c2, u : D // 2 : 2], ident_f[:])
                banks.append(wt)
            return banks

        def w_copy(k, cp, wt, engine):
            dst = w_grp[k][:].rearrange("p d t -> p (d t)").bitcast(F32)
            dst = dst.rearrange("p (q a w) -> p q a w", a=2, w=4)[:, :, cp, :]
            src = wt[:].rearrange("p c u q -> p q (c u)")
            if engine == "v":
                nc.vector.tensor_copy(out=dst, in_=src)
            else:
                nc.scalar.copy(out=dst, in_=src)

        def w_quant(k):
            nc.vector.quantize_mx(
                out=w_codes[:, k, :].bitcast(FP8X4),
                scales=w_scales[:, k, :],
                in_=w_grp[k][:].rearrange("p d t -> p (d t)"),
            )

        ctx.enter_context(tc.manual_schedule())
        transposes(0)
        spread_mu()
        transposes(1)
        centre_only(0)
        regroup(0)
        centre_and_regroup(1)
        wt0 = w_transposes(0)
        w_copy(0, 0, wt0[0], "v")
        w_copy(0, 1, wt0[1], "s")
        wt1 = w_transposes(1)
        w_copy(1, 0, wt1[0], "s")
        w_copy(1, 1, wt1[1], "s")
        transposes(2)
        transposes(3)
        w_quant(0)
        quantise(0)
        w_quant(1)
        for n in range(NP):
            if n + 1 < NP:
                centre_only(2 * n + 2)
                regroup(2 * n + 2)
            if n > 0:
                quantise(n)
            if n + 1 < NP:
                centre_and_regroup(2 * n + 3)
            banks = multiply(n)
            if n == 0:
                transposes(4)
                transposes(5)
            if n + 3 < NP:
                transposes(2 * n + 6)
                transposes(2 * n + 7)
            drain(banks, "svsv" if n == NP - 1 else "ssss")
